import numpy as np
import ml_dtypes


def mxq(x, axis, fmt="e4m3"):
    dtype, down = {"e4m3": (ml_dtypes.float8_e4m3fn, 7), "e5m2": (ml_dtypes.float8_e5m2, 14)}[fmt]
    v = np.moveaxis(np.asarray(x, np.float32).astype(ml_dtypes.bfloat16).astype(np.float64), axis, -1)
    blocks = v.reshape(v.shape[:-1] + (-1, 32))
    amax = np.abs(blocks).max(-1, keepdims=True)
    byte = np.maximum(np.where(amax > 0, np.frexp(amax)[1] - 1 + 127, 0) - down, 1)
    scale = np.exp2(byte - 127.0)
    codes = (blocks / scale).astype(np.float32).astype(dtype).astype(np.float64)
    return np.moveaxis((codes * scale).reshape(v.shape), -1, axis)


WIDE = False


def mx_kscale(k):
    if not WIDE:
        return np.ones(k)
    levels = np.array([10, -10, 5, -5, 0])
    if k % 512:
        return np.exp2(np.random.permutation(np.resize(levels, k // 32))).repeat(32)
    a = np.empty((k // 512, 16))
    for p in range(k // 512):
        a[p, :8] = np.random.permutation(np.resize(levels, 8))
        for g in range(8):
            far = levels[np.abs(levels - a[p, g]) >= 10]
            a[p, g + 8] = far[np.random.randint(len(far))]
    return np.exp2(a.ravel()).repeat(32)


BF16 = ml_dtypes.bfloat16


def bf(x):
    return np.asarray(x, np.float32).astype(BF16)


def f64(x):
    return np.asarray(x).astype(np.float64)


N, C, H, W, HIDDEN, OUT = 8, 512, 16, 16, 512, 256
P = H * W
M = N * P


def leaky_relu(v):
    return np.where(v >= 0.0, v, 0.01 * v)


def setup_inputs():
    s, t = mx_kscale(M), mx_kscale(C)
    strong = np.where(np.random.random((M, M)) * N < 1.0, 1.0, 0.02)
    weight = np.random.random((M, M)) * strong * 2.0 / P
    x = np.random.standard_normal((N, C, H, W)) * 0.25 * np.sqrt(P)
    return {"x": bf(x * t[None, :, None, None] / s.reshape(N, 1, H, W)),
            "weight": bf(weight * s[None, :]),
            "W1": bf(np.random.standard_normal((HIDDEN, C)) * 3.0 / np.sqrt(C) / t[None, :]),
            "b1": bf(np.random.standard_normal(HIDDEN) * 0.2 - 0.4)}


def reference(x, weight, W1, b1):
    nodes = f64(x).transpose(0, 2, 3, 1).reshape(-1, C)
    agg = mxq(f64(weight), 1, "e4m3") @ mxq(nodes, 0, "e4m3")
    return leaky_relu((mxq(agg, 1, "e4m3") @ mxq(f64(W1), 1, "e4m3").T) + f64(b1))

@@ -1,0 +1,211 @@
+from contextlib import ExitStack
+
+import concourse.mybir as mybir
+from concourse.masks import make_identity
+
+F32 = mybir.dt.float32
+BF16 = mybir.dt.bfloat16
+U32 = mybir.dt.uint32
+U8 = mybir.dt.uint8
+FP8X4 = mybir.dt.float8_e4m3fn_x4
+ALU = mybir.AluOpType
+
+P = 128
+PACK = 4
+K_PASS = P * PACK
+BANK = 512
+BANKS = 8
+
+SAMPLES, CHANNELS, PIXELS = 8, 512, 256
+NODES = SAMPLES * PIXELS
+HIDDEN = 512
+SLOPE = 0.01
+
+PASSES = NODES // K_PASS
+GROUPS = CHANNELS // P
+TILES = 2
+ROUNDS = NODES // (TILES * P)
+TILE_CODES = PASSES * P
+
+FLOPS = 2 * NODES * NODES * CHANNELS + 2 * NODES * CHANNELS * HIDDEN
+
+
+def tile_similargcn_pa_kernel(tc, x, weight, W1, b1, out):
+    nc = tc.nc
+    with ExitStack() as ctx:
+        keep = ctx.enter_context(tc.tile_pool(name="keep", bufs=1))
+        raw = ctx.enter_context(tc.tile_pool(name="raw", bufs=ROUNDS))
+        work = ctx.enter_context(tc.tile_pool(name="work", bufs=3))
+        ends = ctx.enter_context(tc.tile_pool(name="ends", bufs=4))
+        psum = ctx.enter_context(tc.psum_pool(name="psum", bufs=BANKS))
+        ctx.enter_context(tc.manual_schedule())
+
+        ident = keep.tile([P, P], F32)
+        make_identity(nc, ident[:])
+        ones = keep.tile([P, P], BF16)
+        nc.gpsimd.memset(ones[:], 1.0)
+        bias_rows = keep.tile([P, HIDDEN], BF16)
+        nc.gpsimd.memset(bias_rows[:], 0.0)
+
+        x_view = x.rearrange("n (p j) h w -> n p j (h w)", j=GROUPS)
+        x_raw = keep.tile([P, SAMPLES * GROUPS * PIXELS], BF16)
+        x_raw_by_pass = x_raw[:].rearrange("p (g j n f) -> p g j n f", g=PASSES, j=GROUPS, n=2)
+        for n in range(SAMPLES):
+            nc.sync.dma_start(out=x_raw_by_pass[:, n // 2, :, n % 2, :], in_=x_view[n])
+        weight_rounds = weight.rearrange("(i p r) k -> i p (r k)", p=P, r=TILES)
+        out_rounds = out.rearrange("(i p r) h -> i p (r h)", p=P, r=TILES)
+        w1_raw = keep.tile([P, GROUPS * CHANNELS], BF16)
+        w_raws = []
+        for i in range(ROUNDS):
+            w_raw = raw.tile([P, TILES * NODES], BF16)
+            nc.sync.dma_start(out=w_raw[:], in_=weight_rounds[i])
+            w_raws.append(w_raw)
+            if i == 0:
+                nc.sync.dma_start(
+                    out=w1_raw[:].rearrange("p (a c) -> p a c", a=GROUPS),
+                    in_=W1.rearrange("(a p) c -> p a c", p=P),
+                )
+                nc.sync.dma_start(out=bias_rows[0:1, :], in_=b1.rearrange("(o h) -> o h", o=1))
+
+        def transpose_words(words, first, step):
+            bank = psum.tile([P, BANK], F32, tag="bank")
+            for q in range(4):
+                nc.tensor.transpose(
+                    out=bank[:, q * P : (q + 1) * P],
+                    in_=words[:, first(q) : first(q) + step * (P - 1) + 1 : step],
+                    identity=ident[:],
+                )
+            return bank
+
+        def pair_up(copy, bank, grouped):
+            copy(
+                out=grouped.bitcast(F32).rearrange("p (a c u) -> p a c u", a=2, u=2),
+                in_=bank[:].rearrange("p (a u c) -> p a c u", a=2, u=2),
+            )
+
+        x_words = x_raw[:].bitcast(F32)
+        x_codes = keep.tile([P, PASSES * CHANNELS], U32, align_bytes=64)
+        x_scales = keep.tile([P, PASSES * CHANNELS], U8, align_bytes=64)
+        for g in range(PASSES):
+            x_grouped = work.tile([P, CHANNELS * PACK], BF16, align_bytes=64)
+            for half, copy in enumerate((nc.scalar.copy, nc.vector.tensor_copy)):
+                bank = transpose_words(
+                    x_words, lambda q: (g * GROUPS + 2 * half + q // 2) * 2 * P + q % 2, 2
+                )
+                pair_up(copy, bank, x_grouped[:, half * 2 * BANK : (half + 1) * 2 * BANK])
+            cols = slice(g * CHANNELS, (g + 1) * CHANNELS)
+            nc.vector.quantize_mx(out=x_codes[:, cols].bitcast(FP8X4), scales=x_scales[:, cols], in_=x_grouped[:])
+
+        w_tiles = {}
+        agg_tiles = {}
+
+        def turn_weight(i):
+            w_words = w_raws[i][:].bitcast(F32)
+            w_grouped = work.tile([P, TILES * NODES], BF16, align_bytes=64)
+            w_codes = work.tile([P, TILES * TILE_CODES], U32, align_bytes=64)
+            w_scales = work.tile([P, TILES * TILE_CODES], U8, align_bytes=64)
+            for b in range(2 * TILES):
+                bank = transpose_words(w_words, lambda q: (2 * b + q // 2) * 2 * P + q % 2, 2)
+                pair_up(nc.scalar.copy, bank, w_grouped[:, b * 2 * BANK : (b + 1) * 2 * BANK])
+            w_tiles[i] = (w_grouped, w_codes, w_scales)
+
+        def quantise_weight(i, r):
+            w_grouped, w_codes, w_scales = w_tiles[i]
+            cols = slice(r * TILE_CODES, (r + 1) * TILE_CODES)
+            nc.vector.quantize_mx(
+                out=w_codes[:, cols].bitcast(FP8X4),
+                scales=w_scales[:, cols],
+                in_=w_grouped[:, r * NODES : (r + 1) * NODES],
+            )
+
+        def aggregate(i, tiles):
+            w_grouped, w_codes, w_scales = w_tiles[i]
+            if i not in agg_tiles:
+                agg_grouped = work.tile([P, TILES * P * PACK], BF16, align_bytes=64)
+                agg_codes = work.tile([P, TILES * P], U32, align_bytes=64)
+                agg_scales = work.tile([P, TILES * P], U8, align_bytes=64)
+                agg_tiles[i] = (agg_grouped, agg_codes, agg_scales)
+            agg_grouped, agg_codes, agg_scales = agg_tiles[i]
+            for r in tiles:
+                agg_bank = psum.tile([P, BANK], F32, tag="bank")
+                for j in range(GROUPS):
+                    for g in range(PASSES):
+                        x_cols = slice(g * CHANNELS + j * P, g * CHANNELS + (j + 1) * P)
+                        w_cols = slice(r * TILE_CODES + g * P, r * TILE_CODES + (g + 1) * P)
+                        nc.tensor.matmul_mx(
+                            out=agg_bank[:, j * P : (j + 1) * P],
+                            lhsT=x_codes[:, x_cols].bitcast(FP8X4),
+                            lhsT_scale=x_scales[:, x_cols],
+                            rhs=w_codes[:, w_cols].bitcast(FP8X4),
+                            rhs_scale=w_scales[:, w_cols],
+                            start=(g == 0),
+                            stop=(g == PASSES - 1),
+                        )
+                values = agg_grouped[:, r * P * PACK : (r + 1) * P * PACK]
+                nc.scalar.copy(
+                    out=values.rearrange("p (m j) -> p m j", j=GROUPS),
+                    in_=agg_bank[:].rearrange("p (j m) -> p m j", j=GROUPS),
+                )
+                nc.vector.quantize_mx(
+                    out=agg_codes[:, r * P : (r + 1) * P].bitcast(FP8X4),
+                    scales=agg_scales[:, r * P : (r + 1) * P],
+                    in_=values,
+                )
+
+        def project(i, r):
+            agg_grouped, agg_codes, agg_scales = agg_tiles[i]
+            out_bank = psum.tile([P, BANK], F32, tag="bank")
+            nc.tensor.matmul_mx(
+                out=out_bank[:],
+                lhsT=agg_codes[:, r * P : (r + 1) * P].bitcast(FP8X4),
+                lhsT_scale=agg_scales[:, r * P : (r + 1) * P],
+                rhs=w1_codes[:].bitcast(FP8X4),
+                rhs_scale=w1_scales[:],
+                start=True,
+                stop=True,
+            )
+            biased = ends.tile([P, HIDDEN], F32)
+            nc.vector.tensor_tensor(out=biased[:], in0=out_bank[:], in1=bias[:], op=ALU.add)
+            return biased
+
+        def leaky_store(biased, i, r):
+            result = ends.tile([P, HIDDEN], F32)
+            nc.vector.scalar_tensor_tensor(
+                out=result[:], in0=biased[:], scalar=SLOPE, in1=biased[:], op0=ALU.mult, op1=ALU.max
+            )
+            nc.sync.dma_start(out=out_rounds[i][:, r * HIDDEN : (r + 1) * HIDDEN], in_=result[:])
+
+        turn_weight(0)
+        for r in range(TILES):
+            quantise_weight(0, r)
+
+        w1_words = w1_raw[:].bitcast(F32)
+        w1_grouped = keep.tile([P, HIDDEN * PACK], BF16, align_bytes=64)
+        w1_codes = keep.tile([P, HIDDEN], U32, align_bytes=64)
+        w1_scales = keep.tile([P, HIDDEN], U8, align_bytes=64)
+        for half, copy in enumerate((nc.scalar.copy, nc.vector.tensor_copy)):
+            bank = transpose_words(w1_words, lambda q: (2 * half + q // 2) * (CHANNELS // 2) + q % 2, 2)
+            pair_up(copy, bank, w1_grouped[:, half * 2 * BANK : (half + 1) * 2 * BANK])
+        nc.vector.quantize_mx(out=w1_codes[:].bitcast(FP8X4), scales=w1_scales[:], in_=w1_grouped[:])
+
+        bias_bank = psum.tile([P, BANK], F32, tag="bank")
+        nc.tensor.matmul(out=bias_bank[:], lhsT=ones[:], rhs=bias_rows[:], start=True, stop=True)
+        bias = keep.tile([P, HIDDEN], F32)
+        nc.vector.tensor_copy(out=bias[:], in_=bias_bank[:])
+
+        aggregate(0, (0, 1))
+        turn_weight(1)
+        for r in range(TILES):
+            quantise_weight(1, r)
+        for i in range(2, ROUNDS + 2):
+            if i < ROUNDS:
+                turn_weight(i)
+                for r in range(TILES):
+                    quantise_weight(i, r)
+            if i - 1 < ROUNDS:
+                aggregate(i - 1, (0,))
+            sums = [project(i - 2, r) for r in range(TILES)]
+            for r in range(TILES):
+                leaky_store(sums[r], i - 2, r)
+            if i - 1 < ROUNDS:
+                aggregate(i - 1, (1,))

@@ -19,6 +19,7 @@ BANKS = 8
 SAMPLES, CHANNELS, PIXELS = 8, 512, 256
 NODES = SAMPLES * PIXELS
 HIDDEN = 512
+HALF = 16
 SLOPE = 0.01
 
 PASSES = NODES // K_PASS
@@ -47,11 +48,11 @@ def tile_similargcn_pa_kernel(tc, x, weight, W1, b1, out):
         bias_rows = keep.tile([P, HIDDEN], BF16)
         nc.gpsimd.memset(bias_rows[:], 0.0)
 
-        x_view = x.rearrange("n (p j) h w -> n p j (h w)", j=GROUPS)
+        x_view = x.rearrange("n (p j) h w -> p n (j h w)", j=GROUPS)
         x_raw = keep.tile([P, SAMPLES * GROUPS * PIXELS], BF16)
-        x_raw_by_pass = x_raw[:].rearrange("p (g j n f) -> p g j n f", g=PASSES, j=GROUPS, n=2)
-        for n in range(SAMPLES):
-            nc.sync.dma_start(out=x_raw_by_pass[:, n // 2, :, n % 2, :], in_=x_view[n])
+        x_raw_by_sample = x_raw[:].rearrange("p (n f) -> p n f", n=SAMPLES)
+        for g in range(PASSES):
+            nc.sync.dma_start(out=x_raw_by_sample[:, 2 * g : 2 * g + 2, :], in_=x_view[:, 2 * g : 2 * g + 2, :])
         weight_rounds = weight.rearrange("(i p r) k -> i p (r k)", p=P, r=TILES)
         out_rounds = out.rearrange("(i p r) h -> i p (r h)", p=P, r=TILES)
         w1_raw = keep.tile([P, GROUPS * CHANNELS], BF16)
@@ -83,14 +84,23 @@ def tile_similargcn_pa_kernel(tc, x, weight, W1, b1, out):
                 in_=bank[:].rearrange("p (a u c) -> p a c u", a=2, u=2),
             )
 
-        x_words = x_raw[:].bitcast(F32)
+        x_sorted = keep.tile([P, SAMPLES * GROUPS * PIXELS], BF16)
+        x_words = x_sorted[:].bitcast(F32)
         x_codes = keep.tile([P, PASSES * CHANNELS], U32, align_bytes=64)
         x_scales = keep.tile([P, PASSES * CHANNELS], U8, align_bytes=64)
         for g in range(PASSES):
+            halves = x_sorted[:, g * 2 * GROUPS * PIXELS : (g + 1) * 2 * GROUPS * PIXELS].rearrange(
+                "p (u j n b e) -> p n u j b e", u=2, j=GROUPS, n=2, e=HALF
+            )
+            for n in range(2):
+                nc.vector.tensor_copy(
+                    out=halves[:, n],
+                    in_=x_raw_by_sample[:, 2 * g + n, :].rearrange("p (j b u e) -> p u j b e", j=GROUPS, u=2, e=HALF),
+                )
             x_grouped = work.tile([P, CHANNELS * PACK], BF16, align_bytes=64)
             for half, copy in enumerate((nc.scalar.copy, nc.vector.tensor_copy)):
                 bank = transpose_words(
-                    x_words, lambda q: (g * GROUPS + 2 * half + q // 2) * 2 * P + q % 2, 2
+                    x_words, lambda q: (g * 2 * GROUPS + (q % 2) * GROUPS + 2 * half + q // 2) * P, 1
                 )
                 pair_up(copy, bank, x_grouped[:, half * 2 * BANK : (half + 1) * 2 * BANK])
             cols = slice(g * CHANNELS, (g + 1) * CHANNELS)
@@ -98,14 +108,23 @@ def tile_similargcn_pa_kernel(tc, x, weight, W1, b1, out):
 
         w_tiles = {}
         agg_tiles = {}
+        sorted_tiles = {}
+
+        def sort_weight(copy, i, r):
+            w_sorted = work.tile([P, NODES], BF16, name="w_sorted_%d" % r)
+            copy(
+                out=w_sorted[:].rearrange("p (u b e) -> p u b e", u=2, e=HALF),
+                in_=w_raws[i][:, r * NODES : (r + 1) * NODES].rearrange("p (b u e) -> p u b e", u=2, e=HALF),
+            )
+            sorted_tiles[i, r] = w_sorted
 
         def turn_weight(i):
-            w_words = w_raws[i][:].bitcast(F32)
             w_grouped = work.tile([P, TILES * NODES], BF16, align_bytes=64)
             w_codes = work.tile([P, TILES * TILE_CODES], U32, align_bytes=64)
             w_scales = work.tile([P, TILES * TILE_CODES], U8, align_bytes=64)
             for b in range(2 * TILES):
-                bank = transpose_words(w_words, lambda q: (2 * b + q // 2) * 2 * P + q % 2, 2)
+                w_words = sorted_tiles[i, b // 2][:].bitcast(F32)
+                bank = transpose_words(w_words, lambda q: ((q % 2) * PASSES + 2 * (b % 2) + q // 2) * P, 1)
                 pair_up(nc.scalar.copy, bank, w_grouped[:, b * 2 * BANK : (b + 1) * 2 * BANK])
             w_tiles[i] = (w_grouped, w_codes, w_scales)
 
@@ -175,6 +194,8 @@ def tile_similargcn_pa_kernel(tc, x, weight, W1, b1, out):
             )
             nc.sync.dma_start(out=out_rounds[i][:, r * HIDDEN : (r + 1) * HIDDEN], in_=result[:])
 
+        sort_weight(nc.vector.tensor_copy, 0, 0)
+        sort_weight(nc.scalar.copy, 0, 1)
         turn_weight(0)
         for r in range(TILES):
             quantise_weight(0, r)
@@ -193,17 +214,25 @@ def tile_similargcn_pa_kernel(tc, x, weight, W1, b1, out):
         bias = keep.tile([P, HIDDEN], F32)
         nc.vector.tensor_copy(out=bias[:], in_=bias_bank[:])
 
+        sort_weight(nc.vector.tensor_copy, 1, 0)
+        sort_weight(nc.scalar.copy, 1, 1)
         aggregate(0, (0, 1))
+        sort_weight(nc.vector.tensor_copy, 2, 0)
         turn_weight(1)
+        sort_weight(nc.scalar.copy, 2, 1)
         for r in range(TILES):
             quantise_weight(1, r)
         for i in range(2, ROUNDS + 2):
+            if i + 1 < ROUNDS:
+                sort_weight(nc.vector.tensor_copy, i + 1, 0)
             if i < ROUNDS:
                 turn_weight(i)
                 for r in range(TILES):
                     quantise_weight(i, r)
             if i - 1 < ROUNDS:
                 aggregate(i - 1, (0,))
+            if i + 1 < ROUNDS:
+                sort_weight(nc.scalar.copy, i + 1, 1)
             sums = [project(i - 2, r) for r in range(TILES)]
             for r in range(TILES):
                 leaky_store(sums[r], i - 2, r)

@@ -19,7 +19,7 @@ BANKS = 8
 SAMPLES, CHANNELS, PIXELS = 8, 512, 256
 NODES = SAMPLES * PIXELS
 HIDDEN = 512
-HALF = 16
+SPLIT_ROUNDS = 2
 SLOPE = 0.01
 
 PASSES = NODES // K_PASS
@@ -59,9 +59,14 @@ def tile_similargcn_pa_kernel(tc, x, weight, W1, b1, out):
         w_raws = []
         for i in range(ROUNDS):
             w_raw = raw.tile([P, TILES * NODES], BF16)
-            nc.sync.dma_start(out=w_raw[:], in_=weight_rounds[i])
+            if i < SPLIT_ROUNDS:
+                for r in range(TILES):
+                    cols = slice(r * NODES, (r + 1) * NODES)
+                    nc.sync.dma_start(out=w_raw[:, cols], in_=weight_rounds[i][:, cols])
+            else:
+                nc.sync.dma_start(out=w_raw[:], in_=weight_rounds[i])
             w_raws.append(w_raw)
-            if i == 0:
+            if i == 1:
                 nc.sync.dma_start(
                     out=w1_raw[:].rearrange("p (a c) -> p a c", a=GROUPS),
                     in_=W1.rearrange("(a p) c -> p a c", p=P),
@@ -84,157 +89,227 @@ def tile_similargcn_pa_kernel(tc, x, weight, W1, b1, out):
                 in_=bank[:].rearrange("p (a u c) -> p a c u", a=2, u=2),
             )
 
-        x_sorted = keep.tile([P, SAMPLES * GROUPS * PIXELS], BF16)
-        x_words = x_sorted[:].bitcast(F32)
+        scalar_copy, vector_copy = nc.scalar.copy, nc.vector.tensor_copy
+
         x_codes = keep.tile([P, PASSES * CHANNELS], U32, align_bytes=64)
         x_scales = keep.tile([P, PASSES * CHANNELS], U8, align_bytes=64)
-        for g in range(PASSES):
-            halves = x_sorted[:, g * 2 * GROUPS * PIXELS : (g + 1) * 2 * GROUPS * PIXELS].rearrange(
-                "p (u j n b e) -> p n u j b e", u=2, j=GROUPS, n=2, e=HALF
-            )
+        x_sorted = [keep.tile([P, 2 * GROUPS * P], F32, name="x_sorted_%d" % g) for g in range(PASSES)]
+        x_groupeds = {}
+
+        def sort_nodes(g):
+            by_sample = x_sorted[g][:].rearrange("p (u j n q) -> p n u j q", u=2, j=GROUPS, n=2)
             for n in range(2):
-                nc.vector.tensor_copy(
-                    out=halves[:, n],
-                    in_=x_raw_by_sample[:, 2 * g + n, :].rearrange("p (j b u e) -> p u j b e", j=GROUPS, u=2, e=HALF),
-                )
+                words = x_raw_by_sample[:, 2 * g + n, :].bitcast(F32)
+                vector_copy(out=by_sample[:, n], in_=words.rearrange("p (j q u) -> p u j q", j=GROUPS, u=2))
+
+        def turn_nodes(g, copies):
             x_grouped = work.tile([P, CHANNELS * PACK], BF16, align_bytes=64)
-            for half, copy in enumerate((nc.scalar.copy, nc.vector.tensor_copy)):
-                bank = transpose_words(
-                    x_words, lambda q: (g * 2 * GROUPS + (q % 2) * GROUPS + 2 * half + q // 2) * P, 1
-                )
+            for half, copy in enumerate(copies):
+                bank = transpose_words(x_sorted[g][:], lambda q: ((q % 2) * GROUPS + 2 * half + q // 2) * P, 1)
                 pair_up(copy, bank, x_grouped[:, half * 2 * BANK : (half + 1) * 2 * BANK])
+            x_groupeds[g] = x_grouped
+
+        def quantise_nodes(g):
             cols = slice(g * CHANNELS, (g + 1) * CHANNELS)
-            nc.vector.quantize_mx(out=x_codes[:, cols].bitcast(FP8X4), scales=x_scales[:, cols], in_=x_grouped[:])
-
-        w_tiles = {}
-        agg_tiles = {}
-        sorted_tiles = {}
-
-        def sort_weight(copy, i, r):
-            w_sorted = work.tile([P, NODES], BF16, name="w_sorted_%d" % r)
-            copy(
-                out=w_sorted[:].rearrange("p (u b e) -> p u b e", u=2, e=HALF),
-                in_=w_raws[i][:, r * NODES : (r + 1) * NODES].rearrange("p (b u e) -> p u b e", u=2, e=HALF),
+            nc.vector.quantize_mx(
+                out=x_codes[:, cols].bitcast(FP8X4), scales=x_scales[:, cols], in_=x_groupeds[g][:]
             )
-            sorted_tiles[i, r] = w_sorted
 
-        def turn_weight(i):
-            w_grouped = work.tile([P, TILES * NODES], BF16, align_bytes=64)
-            w_codes = work.tile([P, TILES * TILE_CODES], U32, align_bytes=64)
-            w_scales = work.tile([P, TILES * TILE_CODES], U8, align_bytes=64)
-            for b in range(2 * TILES):
-                w_words = sorted_tiles[i, b // 2][:].bitcast(F32)
-                bank = transpose_words(w_words, lambda q: ((q % 2) * PASSES + 2 * (b % 2) + q // 2) * P, 1)
-                pair_up(nc.scalar.copy, bank, w_grouped[:, b * 2 * BANK : (b + 1) * 2 * BANK])
-            w_tiles[i] = (w_grouped, w_codes, w_scales)
+        w1_grouped = keep.tile([P, HIDDEN * PACK], BF16, align_bytes=64)
+        w1_codes = keep.tile([P, HIDDEN], U32, align_bytes=64)
+        w1_scales = keep.tile([P, HIDDEN], U8, align_bytes=64)
+        bias = keep.tile([P, HIDDEN], F32)
+
+        def turn_w1(copies):
+            w1_words = w1_raw[:].bitcast(F32)
+            for half, copy in enumerate(copies):
+                bank = transpose_words(w1_words, lambda q: (2 * half + q // 2) * (CHANNELS // 2) + q % 2, 2)
+                pair_up(copy, bank, w1_grouped[:, half * 2 * BANK : (half + 1) * 2 * BANK])
+
+        def quantise_w1():
+            nc.vector.quantize_mx(out=w1_codes[:].bitcast(FP8X4), scales=w1_scales[:], in_=w1_grouped[:])
+
+        def spread_bias():
+            bias_bank = psum.tile([P, BANK], F32, tag="bank")
+            nc.tensor.matmul(out=bias_bank[:], lhsT=ones[:], rhs=bias_rows[:], start=True, stop=True)
+            vector_copy(out=bias[:], in_=bias_bank[:])
+
+        sorteds, w_tiles, agg_tiles, out_banks, biaseds = {}, {}, {}, {}, {}
+
+        def sort_weight(copy, i, r, halves=(0, 1)):
+            if (i, r) not in sorteds:
+                sorteds[i, r] = work.tile([P, NODES // 2], F32, name="w_sorted_%d" % r)
+            first, last = halves[0], halves[-1] + 1
+            words = w_raws[i][:, r * NODES : (r + 1) * NODES].bitcast(F32)
+            copy(
+                out=sorteds[i, r][:].rearrange("p (u q) -> p u q", u=2)[:, :, first * 2 * P : last * 2 * P],
+                in_=words[:, first * BANK : last * BANK].rearrange("p (q u) -> p u q", u=2),
+            )
+
+        def turn_weight(i, r, copies):
+            w_grouped = work.tile([P, NODES], BF16, align_bytes=64, name="w_grouped_%d" % r)
+            w_codes = work.tile([P, TILE_CODES], U32, align_bytes=64, name="w_codes_%d" % r)
+            w_scales = work.tile([P, TILE_CODES], U8, align_bytes=64, name="w_scales_%d" % r)
+            for half, copy in enumerate(copies):
+                if (i, r) in sorteds:
+                    bank = transpose_words(
+                        sorteds[i, r][:], lambda q: ((q % 2) * PASSES + 2 * half + q // 2) * P, 1
+                    )
+                else:
+                    words = w_raws[i][:, r * NODES : (r + 1) * NODES].bitcast(F32)
+                    bank = transpose_words(words, lambda q: (2 * half + q // 2) * 2 * P + q % 2, 2)
+                pair_up(copy, bank, w_grouped[:, half * 2 * BANK : (half + 1) * 2 * BANK])
+            w_tiles[i, r] = (w_grouped, w_codes, w_scales)
 
         def quantise_weight(i, r):
-            w_grouped, w_codes, w_scales = w_tiles[i]
-            cols = slice(r * TILE_CODES, (r + 1) * TILE_CODES)
-            nc.vector.quantize_mx(
-                out=w_codes[:, cols].bitcast(FP8X4),
-                scales=w_scales[:, cols],
-                in_=w_grouped[:, r * NODES : (r + 1) * NODES],
-            )
+            w_grouped, w_codes, w_scales = w_tiles[i, r]
+            nc.vector.quantize_mx(out=w_codes[:].bitcast(FP8X4), scales=w_scales[:], in_=w_grouped[:])
 
-        def aggregate(i, tiles):
-            w_grouped, w_codes, w_scales = w_tiles[i]
-            if i not in agg_tiles:
-                agg_grouped = work.tile([P, TILES * P * PACK], BF16, align_bytes=64)
-                agg_codes = work.tile([P, TILES * P], U32, align_bytes=64)
-                agg_scales = work.tile([P, TILES * P], U8, align_bytes=64)
-                agg_tiles[i] = (agg_grouped, agg_codes, agg_scales)
-            agg_grouped, agg_codes, agg_scales = agg_tiles[i]
-            for r in tiles:
-                agg_bank = psum.tile([P, BANK], F32, tag="bank")
-                for j in range(GROUPS):
-                    for g in range(PASSES):
-                        x_cols = slice(g * CHANNELS + j * P, g * CHANNELS + (j + 1) * P)
-                        w_cols = slice(r * TILE_CODES + g * P, r * TILE_CODES + (g + 1) * P)
-                        nc.tensor.matmul_mx(
-                            out=agg_bank[:, j * P : (j + 1) * P],
-                            lhsT=x_codes[:, x_cols].bitcast(FP8X4),
-                            lhsT_scale=x_scales[:, x_cols],
-                            rhs=w_codes[:, w_cols].bitcast(FP8X4),
-                            rhs_scale=w_scales[:, w_cols],
-                            start=(g == 0),
-                            stop=(g == PASSES - 1),
-                        )
-                values = agg_grouped[:, r * P * PACK : (r + 1) * P * PACK]
-                nc.scalar.copy(
-                    out=values.rearrange("p (m j) -> p m j", j=GROUPS),
-                    in_=agg_bank[:].rearrange("p (j m) -> p m j", j=GROUPS),
-                )
-                nc.vector.quantize_mx(
-                    out=agg_codes[:, r * P : (r + 1) * P].bitcast(FP8X4),
-                    scales=agg_scales[:, r * P : (r + 1) * P],
-                    in_=values,
-                )
+        def aggregate(i, r):
+            w_grouped, w_codes, w_scales = w_tiles[i, r]
+            agg_grouped = work.tile([P, P * PACK], BF16, align_bytes=64, name="agg_grouped_%d" % r)
+            agg_codes = work.tile([P, P], U32, align_bytes=64, name="agg_codes_%d" % r)
+            agg_scales = work.tile([P, P], U8, align_bytes=64, name="agg_scales_%d" % r)
+            agg_bank = psum.tile([P, BANK], F32, tag="bank")
+            for j in range(GROUPS):
+                for g in range(PASSES):
+                    x_cols = slice(g * CHANNELS + j * P, g * CHANNELS + (j + 1) * P)
+                    w_cols = slice(g * P, (g + 1) * P)
+                    nc.tensor.matmul_mx(
+                        out=agg_bank[:, j * P : (j + 1) * P],
+                        lhsT=x_codes[:, x_cols].bitcast(FP8X4),
+                        lhsT_scale=x_scales[:, x_cols],
+                        rhs=w_codes[:, w_cols].bitcast(FP8X4),
+                        rhs_scale=w_scales[:, w_cols],
+                        start=(g == 0),
+                        stop=(g == PASSES - 1),
+                    )
+            scalar_copy(
+                out=agg_grouped[:].rearrange("p (m j) -> p m j", j=GROUPS),
+                in_=agg_bank[:].rearrange("p (j m) -> p m j", j=GROUPS),
+            )
+            agg_tiles[i, r] = (agg_grouped, agg_codes, agg_scales)
+
+        def quantise_agg(i, r):
+            agg_grouped, agg_codes, agg_scales = agg_tiles[i, r]
+            nc.vector.quantize_mx(out=agg_codes[:].bitcast(FP8X4), scales=agg_scales[:], in_=agg_grouped[:])
 
         def project(i, r):
-            agg_grouped, agg_codes, agg_scales = agg_tiles[i]
+            agg_grouped, agg_codes, agg_scales = agg_tiles[i, r]
             out_bank = psum.tile([P, BANK], F32, tag="bank")
             nc.tensor.matmul_mx(
                 out=out_bank[:],
-                lhsT=agg_codes[:, r * P : (r + 1) * P].bitcast(FP8X4),
-                lhsT_scale=agg_scales[:, r * P : (r + 1) * P],
+                lhsT=agg_codes[:].bitcast(FP8X4),
+                lhsT_scale=agg_scales[:],
                 rhs=w1_codes[:].bitcast(FP8X4),
                 rhs_scale=w1_scales[:],
                 start=True,
                 stop=True,
             )
-            biased = ends.tile([P, HIDDEN], F32)
-            nc.vector.tensor_tensor(out=biased[:], in0=out_bank[:], in1=bias[:], op=ALU.add)
-            return biased
+            out_banks[i, r] = out_bank
 
-        def leaky_store(biased, i, r):
+        def add_bias(i, r):
+            biased = ends.tile([P, HIDDEN], F32)
+            nc.vector.tensor_tensor(out=biased[:], in0=out_banks[i, r][:], in1=bias[:], op=ALU.add)
+            biaseds[i, r] = biased
+
+        def leaky_store(i, r):
+            biased = biaseds[i, r]
             result = ends.tile([P, HIDDEN], F32)
             nc.vector.scalar_tensor_tensor(
                 out=result[:], in0=biased[:], scalar=SLOPE, in1=biased[:], op0=ALU.mult, op1=ALU.max
             )
             nc.sync.dma_start(out=out_rounds[i][:, r * HIDDEN : (r + 1) * HIDDEN], in_=result[:])
 
-        sort_weight(nc.vector.tensor_copy, 0, 0)
-        sort_weight(nc.scalar.copy, 0, 1)
-        turn_weight(0)
-        for r in range(TILES):
-            quantise_weight(0, r)
+        last = ROUNDS
 
-        w1_words = w1_raw[:].bitcast(F32)
-        w1_grouped = keep.tile([P, HIDDEN * PACK], BF16, align_bytes=64)
-        w1_codes = keep.tile([P, HIDDEN], U32, align_bytes=64)
-        w1_scales = keep.tile([P, HIDDEN], U8, align_bytes=64)
-        for half, copy in enumerate((nc.scalar.copy, nc.vector.tensor_copy)):
-            bank = transpose_words(w1_words, lambda q: (2 * half + q // 2) * (CHANNELS // 2) + q % 2, 2)
-            pair_up(copy, bank, w1_grouped[:, half * 2 * BANK : (half + 1) * 2 * BANK])
-        nc.vector.quantize_mx(out=w1_codes[:].bitcast(FP8X4), scales=w1_scales[:], in_=w1_grouped[:])
+        def sort_first(i):
+            if i < last:
+                sort_weight(vector_copy, i, 0)
 
-        bias_bank = psum.tile([P, BANK], F32, tag="bank")
-        nc.tensor.matmul(out=bias_bank[:], lhsT=ones[:], rhs=bias_rows[:], start=True, stop=True)
-        bias = keep.tile([P, HIDDEN], F32)
-        nc.vector.tensor_copy(out=bias[:], in_=bias_bank[:])
+        def sort_second(i, half):
+            if i < last:
+                sort_weight(scalar_copy, i, 1, (half,))
 
-        sort_weight(nc.vector.tensor_copy, 1, 0)
-        sort_weight(nc.scalar.copy, 1, 1)
-        aggregate(0, (0, 1))
-        sort_weight(nc.vector.tensor_copy, 2, 0)
-        turn_weight(1)
-        sort_weight(nc.scalar.copy, 2, 1)
-        for r in range(TILES):
-            quantise_weight(1, r)
-        for i in range(2, ROUNDS + 2):
-            if i + 1 < ROUNDS:
-                sort_weight(nc.vector.tensor_copy, i + 1, 0)
-            if i < ROUNDS:
-                turn_weight(i)
-                for r in range(TILES):
-                    quantise_weight(i, r)
-            if i - 1 < ROUNDS:
-                aggregate(i - 1, (0,))
-            if i + 1 < ROUNDS:
-                sort_weight(nc.scalar.copy, i + 1, 1)
-            sums = [project(i - 2, r) for r in range(TILES)]
-            for r in range(TILES):
-                leaky_store(sums[r], i - 2, r)
-            if i - 1 < ROUNDS:
-                aggregate(i - 1, (1,))
+        sort_nodes(0)
+        sort_nodes(1)
+        for g in range(PASSES - 1):
+            turn_nodes(g, (scalar_copy, scalar_copy))
+            if g + 2 < PASSES:
+                sort_nodes(g + 2)
+            quantise_nodes(g)
+        turn_nodes(PASSES - 1, (scalar_copy, vector_copy))
+        quantise_nodes(PASSES - 1)
+        turn_weight(0, 0, (scalar_copy, scalar_copy))
+        turn_weight(0, 1, (scalar_copy, scalar_copy))
+        quantise_weight(0, 0)
+        sort_first(1)
+        quantise_weight(0, 1)
+        sort_second(1, 0)
+        aggregate(0, 0)
+        sort_second(1, 1)
+        aggregate(0, 1)
+        quantise_agg(0, 0)
+        turn_weight(1, 0, (scalar_copy, scalar_copy))
+        turn_weight(1, 1, (scalar_copy, scalar_copy))
+        sort_first(2)
+        sort_second(2, 0)
+        quantise_agg(0, 1)
+        turn_w1((vector_copy, vector_copy))
+        spread_bias()
+        quantise_weight(1, 0)
+        quantise_w1()
+        quantise_weight(1, 1)
+        sort_second(2, 1)
+        turn_weight(2, 0, (scalar_copy, scalar_copy))
+        turn_weight(2, 1, (scalar_copy, scalar_copy))
+        sort_first(3)
+        aggregate(1, 0)
+        quantise_agg(1, 0)
+        sort_second(3, 0)
+        aggregate(1, 1)
+        quantise_weight(2, 0)
+        project(0, 0)
+        project(0, 1)
+        add_bias(0, 0)
+        quantise_weight(2, 1)
+
+        for i in range(3, last):
+            sort_second(i, 1)
+            turn_weight(i, 0, (scalar_copy, scalar_copy))
+            turn_weight(i, 1, (scalar_copy, scalar_copy))
+            quantise_agg(i - 2, 1)
+            add_bias(i - 3, 1)
+            leaky_store(i - 3, 0)
+            quantise_weight(i, 0)
+            leaky_store(i - 3, 1)
+            quantise_weight(i, 1)
+            aggregate(i - 1, 0)
+            quantise_agg(i - 1, 0)
+            sort_first(i + 1)
+            sort_second(i + 1, 0)
+            aggregate(i - 1, 1)
+            project(i - 2, 0)
+            project(i - 2, 1)
+            add_bias(i - 2, 0)
+
+        quantise_agg(last - 2, 1)
+        add_bias(last - 3, 1)
+        leaky_store(last - 3, 0)
+        leaky_store(last - 3, 1)
+        aggregate(last - 1, 0)
+        project(last - 2, 0)
+        project(last - 2, 1)
+        quantise_agg(last - 1, 0)
+        add_bias(last - 2, 0)
+        add_bias(last - 2, 1)
+        aggregate(last - 1, 1)
+        project(last - 1, 0)
+        leaky_store(last - 2, 0)
+        quantise_agg(last - 1, 1)
+        leaky_store(last - 2, 1)
+        add_bias(last - 1, 0)
+        project(last - 1, 1)
+        add_bias(last - 1, 1)
+        leaky_store(last - 1, 0)
+        leaky_store(last - 1, 1)

@@ -47,6 +47,13 @@ def tile_similargcn_pa_kernel(tc, x, weight, W1, b1, out):
         nc.gpsimd.memset(ones[:], 1.0)
         bias_rows = keep.tile([P, HIDDEN], BF16)
         nc.gpsimd.memset(bias_rows[:], 0.0)
+        warm_rows = keep.tile([P, BANK], BF16)
+        nc.gpsimd.memset(warm_rows[:], 1.0)
+
+        def keep_warm(count):
+            warm_bank = psum.tile([P, BANK], F32, tag="bank")
+            for n in range(count):
+                nc.tensor.matmul(out=warm_bank[:], lhsT=ones[:], rhs=warm_rows[:], start=True, stop=True)
 
         x_view = x.rearrange("n (p j) h w -> p n (j h w)", j=GROUPS)
         x_raw = keep.tile([P, SAMPLES * GROUPS * PIXELS], BF16)
@@ -231,17 +238,22 @@ def tile_similargcn_pa_kernel(tc, x, weight, W1, b1, out):
             if i < last:
                 sort_weight(scalar_copy, i, 1, (half,))
 
+        keep_warm(6)
         sort_nodes(0)
         sort_nodes(1)
         for g in range(PASSES - 1):
             turn_nodes(g, (scalar_copy, scalar_copy))
+            keep_warm(1)
             if g + 2 < PASSES:
                 sort_nodes(g + 2)
             quantise_nodes(g)
         turn_nodes(PASSES - 1, (scalar_copy, vector_copy))
+        keep_warm(1)
         quantise_nodes(PASSES - 1)
         turn_weight(0, 0, (scalar_copy, scalar_copy))
+        keep_warm(1)
         turn_weight(0, 1, (scalar_copy, scalar_copy))
+        keep_warm(2)
         quantise_weight(0, 0)
         sort_first(1)
         quantise_weight(0, 1)

@@ -19,6 +19,7 @@ BANKS = 8
 SAMPLES, CHANNELS, PIXELS = 8, 512, 256
 NODES = SAMPLES * PIXELS
 HIDDEN = 512
+FIRST_STEP = 3
 SPLIT_ROUNDS = 2
 SLOPE = 0.01
 
@@ -73,7 +74,7 @@ def tile_similargcn_pa_kernel(tc, x, weight, W1, b1, out):
             else:
                 nc.sync.dma_start(out=w_raw[:], in_=weight_rounds[i])
             w_raws.append(w_raw)
-            if i == 1:
+            if i == 0:
                 nc.sync.dma_start(
                     out=w1_raw[:].rearrange("p (a c) -> p a c", a=GROUPS),
                     in_=W1.rearrange("(a p) c -> p a c", p=P),
@@ -174,9 +175,12 @@ def tile_similargcn_pa_kernel(tc, x, weight, W1, b1, out):
 
         def aggregate(i, r):
             w_grouped, w_codes, w_scales = w_tiles[i, r]
-            agg_grouped = work.tile([P, P * PACK], BF16, align_bytes=64, name="agg_grouped_%d" % r)
-            agg_codes = work.tile([P, P], U32, align_bytes=64, name="agg_codes_%d" % r)
-            agg_scales = work.tile([P, P], U8, align_bytes=64, name="agg_scales_%d" % r)
+            if i not in agg_tiles:
+                agg_grouped = work.tile([P, TILES * P * PACK], BF16, align_bytes=64)
+                agg_codes = work.tile([P, TILES * P], U32, align_bytes=64)
+                agg_scales = work.tile([P, TILES * P], U8, align_bytes=64)
+                agg_tiles[i] = (agg_grouped, agg_codes, agg_scales)
+            agg_grouped, agg_codes, agg_scales = agg_tiles[i]
             agg_bank = psum.tile([P, BANK], F32, tag="bank")
             for j in range(GROUPS):
                 for g in range(PASSES):
@@ -192,22 +196,27 @@ def tile_similargcn_pa_kernel(tc, x, weight, W1, b1, out):
                         stop=(g == PASSES - 1),
                     )
             scalar_copy(
-                out=agg_grouped[:].rearrange("p (m j) -> p m j", j=GROUPS),
+                out=agg_grouped[:, r * BANK : (r + 1) * BANK].rearrange("p (m j) -> p m j", j=GROUPS),
                 in_=agg_bank[:].rearrange("p (j m) -> p m j", j=GROUPS),
             )
-            agg_tiles[i, r] = (agg_grouped, agg_codes, agg_scales)
 
-        def quantise_agg(i, r):
-            agg_grouped, agg_codes, agg_scales = agg_tiles[i, r]
-            nc.vector.quantize_mx(out=agg_codes[:].bitcast(FP8X4), scales=agg_scales[:], in_=agg_grouped[:])
+        def quantise_agg(i, first=0, count=TILES):
+            agg_grouped, agg_codes, agg_scales = agg_tiles[i]
+            cols = slice(first * P, (first + count) * P)
+            nc.vector.quantize_mx(
+                out=agg_codes[:, cols].bitcast(FP8X4),
+                scales=agg_scales[:, cols],
+                in_=agg_grouped[:, first * BANK : (first + count) * BANK],
+            )
 
         def project(i, r):
-            agg_grouped, agg_codes, agg_scales = agg_tiles[i, r]
+            agg_grouped, agg_codes, agg_scales = agg_tiles[i]
+            cols = slice(r * P, (r + 1) * P)
             out_bank = psum.tile([P, BANK], F32, tag="bank")
             nc.tensor.matmul_mx(
                 out=out_bank[:],
-                lhsT=agg_codes[:].bitcast(FP8X4),
-                lhsT_scale=agg_scales[:],
+                lhsT=agg_codes[:, cols].bitcast(FP8X4),
+                lhsT_scale=agg_scales[:, cols],
                 rhs=w1_codes[:].bitcast(FP8X4),
                 rhs_scale=w1_scales[:],
                 start=True,
@@ -216,27 +225,31 @@ def tile_similargcn_pa_kernel(tc, x, weight, W1, b1, out):
             out_banks[i, r] = out_bank
 
         def add_bias(i, r):
-            biased = ends.tile([P, HIDDEN], F32)
-            nc.vector.tensor_tensor(out=biased[:], in0=out_banks[i, r][:], in1=bias[:], op=ALU.add)
-            biaseds[i, r] = biased
-
-        def leaky_store(i, r):
-            biased = biaseds[i, r]
-            result = ends.tile([P, HIDDEN], F32)
-            nc.vector.scalar_tensor_tensor(
-                out=result[:], in0=biased[:], scalar=SLOPE, in1=biased[:], op0=ALU.mult, op1=ALU.max
+            if i not in biaseds:
+                biaseds[i] = ends.tile([P, TILES * HIDDEN], F32, name="biased")
+            nc.vector.tensor_tensor(
+                out=biaseds[i][:, r * HIDDEN : (r + 1) * HIDDEN], in0=out_banks[i, r][:], in1=bias[:], op=ALU.add
             )
-            nc.sync.dma_start(out=out_rounds[i][:, r * HIDDEN : (r + 1) * HIDDEN], in_=result[:])
+
+        def leaky_store(i, first=0, count=TILES):
+            cols = slice(first * HIDDEN, (first + count) * HIDDEN)
+            biased = biaseds[i][:, cols]
+            result = ends.tile([P, TILES * HIDDEN], F32)
+            nc.vector.scalar_tensor_tensor(
+                out=result[:, cols], in0=biased, scalar=SLOPE, in1=biased, op0=ALU.mult, op1=ALU.max
+            )
+            nc.sync.dma_start(out=out_rounds[i][:, cols], in_=result[:, cols])
 
         last = ROUNDS
 
-        def sort_first(i):
+        def sort_round(i):
             if i < last:
                 sort_weight(vector_copy, i, 0)
+                sort_weight(vector_copy if i < FIRST_STEP + 1 else scalar_copy, i, 1)
 
-        def sort_second(i, half):
-            if i < last:
-                sort_weight(scalar_copy, i, 1, (half,))
+        def turn_round(i):
+            turn_weight(i, 0, (scalar_copy, scalar_copy))
+            turn_weight(i, 1, (scalar_copy, scalar_copy))
 
         keep_warm(6)
         sort_nodes(0)
@@ -253,75 +266,65 @@ def tile_similargcn_pa_kernel(tc, x, weight, W1, b1, out):
         turn_weight(0, 0, (scalar_copy, scalar_copy))
         keep_warm(1)
         turn_weight(0, 1, (scalar_copy, scalar_copy))
-        keep_warm(2)
+        keep_warm(1)
         quantise_weight(0, 0)
-        sort_first(1)
-        quantise_weight(0, 1)
-        sort_second(1, 0)
-        aggregate(0, 0)
-        sort_second(1, 1)
-        aggregate(0, 1)
-        quantise_agg(0, 0)
-        turn_weight(1, 0, (scalar_copy, scalar_copy))
-        turn_weight(1, 1, (scalar_copy, scalar_copy))
-        sort_first(2)
-        sort_second(2, 0)
-        quantise_agg(0, 1)
-        turn_w1((vector_copy, vector_copy))
+        turn_w1((scalar_copy, scalar_copy))
         spread_bias()
-        quantise_weight(1, 0)
+        sort_weight(vector_copy, 1, 0)
+        quantise_weight(0, 1)
+        sort_weight(vector_copy, 1, 1)
+        aggregate(0, 0)
         quantise_w1()
+        aggregate(0, 1)
+        turn_round(1)
+        sort_weight(vector_copy, 2, 0)
+        quantise_agg(0)
+        sort_weight(vector_copy, 2, 1)
+        quantise_weight(1, 0)
         quantise_weight(1, 1)
-        sort_second(2, 1)
-        turn_weight(2, 0, (scalar_copy, scalar_copy))
-        turn_weight(2, 1, (scalar_copy, scalar_copy))
-        sort_first(3)
-        aggregate(1, 0)
-        quantise_agg(1, 0)
-        sort_second(3, 0)
-        aggregate(1, 1)
-        quantise_weight(2, 0)
+        turn_round(2)
         project(0, 0)
         project(0, 1)
         add_bias(0, 0)
+        add_bias(0, 1)
+        aggregate(1, 0)
+        sort_round(3)
+        aggregate(1, 1)
+        quantise_weight(2, 0)
+        leaky_store(0)
         quantise_weight(2, 1)
+        sort_round(4)
 
-        for i in range(3, last):
-            sort_second(i, 1)
-            turn_weight(i, 0, (scalar_copy, scalar_copy))
-            turn_weight(i, 1, (scalar_copy, scalar_copy))
-            quantise_agg(i - 2, 1)
-            add_bias(i - 3, 1)
-            leaky_store(i - 3, 0)
+        for i in range(FIRST_STEP, last):
+            turn_round(i)
+            if i > FIRST_STEP:
+                leaky_store(i - 3)
+            quantise_agg(i - 2)
+            sort_round(i + 2)
             quantise_weight(i, 0)
-            leaky_store(i - 3, 1)
             quantise_weight(i, 1)
             aggregate(i - 1, 0)
-            quantise_agg(i - 1, 0)
-            sort_first(i + 1)
-            sort_second(i + 1, 0)
-            aggregate(i - 1, 1)
             project(i - 2, 0)
             project(i - 2, 1)
+            aggregate(i - 1, 1)
             add_bias(i - 2, 0)
+            add_bias(i - 2, 1)
 
-        quantise_agg(last - 2, 1)
-        add_bias(last - 3, 1)
-        leaky_store(last - 3, 0)
-        leaky_store(last - 3, 1)
+        leaky_store(last - 3)
+        quantise_agg(last - 2)
         aggregate(last - 1, 0)
         project(last - 2, 0)
         project(last - 2, 1)
-        quantise_agg(last - 1, 0)
+        aggregate(last - 1, 1)
+        quantise_agg(last - 1, 0, 1)
         add_bias(last - 2, 0)
         add_bias(last - 2, 1)
-        aggregate(last - 1, 1)
         project(last - 1, 0)
-        leaky_store(last - 2, 0)
-        quantise_agg(last - 1, 1)
-        leaky_store(last - 2, 1)
-        add_bias(last - 1, 0)
+        leaky_store(last - 2, 0, 1)
+        quantise_agg(last - 1, 1, 1)
         project(last - 1, 1)
+        leaky_store(last - 2, 1, 1)
+        add_bias(last - 1, 0)
+        leaky_store(last - 1, 0, 1)
         add_bias(last - 1, 1)
-        leaky_store(last - 1, 0)
-        leaky_store(last - 1, 1)
+        leaky_store(last - 1, 1, 1)

@@ -38,7 +38,8 @@ def tile_similargcn_pa_kernel(tc, x, weight, W1, b1, out):
         keep = ctx.enter_context(tc.tile_pool(name="keep", bufs=1))
         raw = ctx.enter_context(tc.tile_pool(name="raw", bufs=ROUNDS))
         work = ctx.enter_context(tc.tile_pool(name="work", bufs=3))
-        ends = ctx.enter_context(tc.tile_pool(name="ends", bufs=4))
+        ends = ctx.enter_context(tc.tile_pool(name="ends", bufs=3))
+        results = ctx.enter_context(tc.tile_pool(name="results", bufs=6))
         psum = ctx.enter_context(tc.psum_pool(name="psum", bufs=BANKS))
         ctx.enter_context(tc.manual_schedule())
 
@@ -47,7 +48,7 @@ def tile_similargcn_pa_kernel(tc, x, weight, W1, b1, out):
         ones = keep.tile([P, P], BF16)
         nc.gpsimd.memset(ones[:], 1.0)
         bias_rows = keep.tile([P, HIDDEN], BF16)
-        nc.gpsimd.memset(bias_rows[:], 0.0)
+        nc.vector.memset(bias_rows[:], 0.0)
         warm_rows = keep.tile([P, BANK], BF16)
         nc.gpsimd.memset(warm_rows[:], 1.0)
 
@@ -61,6 +62,8 @@ def tile_similargcn_pa_kernel(tc, x, weight, W1, b1, out):
         x_raw_by_sample = x_raw[:].rearrange("p (n f) -> p n f", n=SAMPLES)
         for g in range(PASSES):
             nc.sync.dma_start(out=x_raw_by_sample[:, 2 * g : 2 * g + 2, :], in_=x_view[:, 2 * g : 2 * g + 2, :])
+            if g == 0:
+                nc.sync.dma_start(out=bias_rows[0:1, :], in_=b1.rearrange("(o h) -> o h", o=1))
         weight_rounds = weight.rearrange("(i p r) k -> i p (r k)", p=P, r=TILES)
         out_rounds = out.rearrange("(i p r) h -> i p (r h)", p=P, r=TILES)
         w1_raw = keep.tile([P, GROUPS * CHANNELS], BF16)
@@ -79,7 +82,6 @@ def tile_similargcn_pa_kernel(tc, x, weight, W1, b1, out):
                     out=w1_raw[:].rearrange("p (a c) -> p a c", a=GROUPS),
                     in_=W1.rearrange("(a p) c -> p a c", p=P),
                 )
-                nc.sync.dma_start(out=bias_rows[0:1, :], in_=b1.rearrange("(o h) -> o h", o=1))
 
         def transpose_words(words, first, step):
             bank = psum.tile([P, BANK], F32, tag="bank")
@@ -105,10 +107,11 @@ def tile_similargcn_pa_kernel(tc, x, weight, W1, b1, out):
         x_groupeds = {}
 
         def sort_nodes(g):
-            by_sample = x_sorted[g][:].rearrange("p (u j n q) -> p n u j q", u=2, j=GROUPS, n=2)
-            for n in range(2):
-                words = x_raw_by_sample[:, 2 * g + n, :].bitcast(F32)
-                vector_copy(out=by_sample[:, n], in_=words.rearrange("p (j q u) -> p u j q", j=GROUPS, u=2))
+            words = x_raw[:, g * 2 * GROUPS * PIXELS : (g + 1) * 2 * GROUPS * PIXELS].bitcast(F32)
+            vector_copy(
+                out=x_sorted[g][:].rearrange("p (u j n q) -> p n u j q", u=2, j=GROUPS, n=2),
+                in_=words.rearrange("p (n j q u) -> p n u j q", n=2, j=GROUPS, u=2),
+            )
 
         def turn_nodes(g, copies):
             x_grouped = work.tile([P, CHANNELS * PACK], BF16, align_bytes=64)
@@ -231,14 +234,25 @@ def tile_similargcn_pa_kernel(tc, x, weight, W1, b1, out):
                 out=biaseds[i][:, r * HIDDEN : (r + 1) * HIDDEN], in0=out_banks[i, r][:], in1=bias[:], op=ALU.add
             )
 
-        def leaky_store(i, first=0, count=TILES):
-            cols = slice(first * HIDDEN, (first + count) * HIDDEN)
+        def leaky_store(i, r):
+            cols = slice(r * HIDDEN, (r + 1) * HIDDEN)
             biased = biaseds[i][:, cols]
-            result = ends.tile([P, TILES * HIDDEN], F32)
+            result = results.tile([P, HIDDEN], F32)
             nc.vector.scalar_tensor_tensor(
-                out=result[:, cols], in0=biased, scalar=SLOPE, in1=biased, op0=ALU.mult, op1=ALU.max
+                out=result[:], in0=biased, scalar=SLOPE, in1=biased, op0=ALU.mult, op1=ALU.max
             )
-            nc.sync.dma_start(out=out_rounds[i][:, cols], in_=result[:, cols])
+            nc.sync.dma_start(out=out_rounds[i][:, cols], in_=result[:])
+
+        def leaky_store_aside(i, r):
+            cols = slice(r * HIDDEN, (r + 1) * HIDDEN)
+            biased = biaseds[i][:, cols]
+            lift = ends.tile([P, HIDDEN], F32)
+            nc.scalar.activation(
+                out=lift[:], in_=biased, func=mybir.ActivationFunctionType.Relu, scale=SLOPE - 1.0
+            )
+            result = results.tile([P, HIDDEN], F32)
+            nc.gpsimd.tensor_tensor(out=result[:], in0=biased, in1=lift[:], op=ALU.add)
+            nc.sync.dma_start(out=out_rounds[i][:, cols], in_=result[:])
 
         last = ROUNDS
 
@@ -256,7 +270,10 @@ def tile_similargcn_pa_kernel(tc, x, weight, W1, b1, out):
         sort_nodes(1)
         for g in range(PASSES - 1):
             turn_nodes(g, (scalar_copy, scalar_copy))
-            keep_warm(1)
+            if g == 0:
+                spread_bias()
+            else:
+                keep_warm(1)
             if g + 2 < PASSES:
                 sort_nodes(g + 2)
             quantise_nodes(g)
@@ -269,7 +286,6 @@ def tile_similargcn_pa_kernel(tc, x, weight, W1, b1, out):
         keep_warm(1)
         quantise_weight(0, 0)
         turn_w1((scalar_copy, scalar_copy))
-        spread_bias()
         sort_weight(vector_copy, 1, 0)
         quantise_weight(0, 1)
         sort_weight(vector_copy, 1, 1)
@@ -291,15 +307,14 @@ def tile_similargcn_pa_kernel(tc, x, weight, W1, b1, out):
         sort_round(3)
         aggregate(1, 1)
         quantise_weight(2, 0)
-        leaky_store(0)
-        quantise_weight(2, 1)
         sort_round(4)
+        quantise_weight(2, 1)
 
         for i in range(FIRST_STEP, last):
             turn_round(i)
-            if i > FIRST_STEP:
-                leaky_store(i - 3)
+            leaky_store(i - 3, 0)
             quantise_agg(i - 2)
+            leaky_store(i - 3, 1)
             sort_round(i + 2)
             quantise_weight(i, 0)
             quantise_weight(i, 1)
@@ -310,21 +325,22 @@ def tile_similargcn_pa_kernel(tc, x, weight, W1, b1, out):
             add_bias(i - 2, 0)
             add_bias(i - 2, 1)
 
-        leaky_store(last - 3)
+        leaky_store(last - 3, 0)
         quantise_agg(last - 2)
+        leaky_store_aside(last - 3, 1)
         aggregate(last - 1, 0)
         project(last - 2, 0)
         project(last - 2, 1)
-        aggregate(last - 1, 1)
         quantise_agg(last - 1, 0, 1)
         add_bias(last - 2, 0)
+        leaky_store_aside(last - 2, 0)
+        aggregate(last - 1, 1)
         add_bias(last - 2, 1)
+        leaky_store(last - 2, 1)
         project(last - 1, 0)
-        leaky_store(last - 2, 0, 1)
         quantise_agg(last - 1, 1, 1)
-        project(last - 1, 1)
-        leaky_store(last - 2, 1, 1)
         add_bias(last - 1, 0)
-        leaky_store(last - 1, 0, 1)
+        project(last - 1, 1)
+        leaky_store(last - 1, 0)
         add_bias(last - 1, 1)
-        leaky_store(last - 1, 1, 1)
+        leaky_store(last - 1, 1)

@@ -278,12 +278,10 @@ def tile_similargcn_pa_kernel(tc, x, weight, W1, b1, out):
                 sort_nodes(g + 2)
             quantise_nodes(g)
         turn_nodes(PASSES - 1, (scalar_copy, vector_copy))
-        keep_warm(1)
         quantise_nodes(PASSES - 1)
         turn_weight(0, 0, (scalar_copy, scalar_copy))
         keep_warm(1)
         turn_weight(0, 1, (scalar_copy, scalar_copy))
-        keep_warm(1)
         quantise_weight(0, 0)
         turn_w1((scalar_copy, scalar_copy))
         sort_weight(vector_copy, 1, 0)
@@ -327,20 +325,20 @@ def tile_similargcn_pa_kernel(tc, x, weight, W1, b1, out):
 
         leaky_store(last - 3, 0)
         quantise_agg(last - 2)
-        leaky_store_aside(last - 3, 1)
+        leaky_store(last - 3, 1)
         aggregate(last - 1, 0)
         project(last - 2, 0)
         project(last - 2, 1)
-        quantise_agg(last - 1, 0, 1)
         add_bias(last - 2, 0)
-        leaky_store_aside(last - 2, 0)
-        aggregate(last - 1, 1)
+        quantise_agg(last - 1, 0, 1)
         add_bias(last - 2, 1)
-        leaky_store(last - 2, 1)
+        leaky_store(last - 2, 0)
+        aggregate(last - 1, 1)
         project(last - 1, 0)
         quantise_agg(last - 1, 1, 1)
         add_bias(last - 1, 0)
         project(last - 1, 1)
+        leaky_store(last - 2, 1)
         leaky_store(last - 1, 0)
         add_bias(last - 1, 1)
         leaky_store(last - 1, 1)

@@ -43,19 +43,17 @@ def tile_similargcn_pa_kernel(tc, x, weight, W1, b1, out):
         psum = ctx.enter_context(tc.psum_pool(name="psum", bufs=BANKS))
         ctx.enter_context(tc.manual_schedule())
 
+        ones = keep.tile([P, BANK], BF16)
+        nc.gpsimd.memset(ones[:], 1.0)
         ident = keep.tile([P, P], F32)
         make_identity(nc, ident[:])
-        ones = keep.tile([P, P], BF16)
-        nc.gpsimd.memset(ones[:], 1.0)
         bias_rows = keep.tile([P, HIDDEN], BF16)
         nc.vector.memset(bias_rows[:], 0.0)
-        warm_rows = keep.tile([P, BANK], BF16)
-        nc.gpsimd.memset(warm_rows[:], 1.0)
 
         def keep_warm(count):
             warm_bank = psum.tile([P, BANK], F32, tag="bank")
             for n in range(count):
-                nc.tensor.matmul(out=warm_bank[:], lhsT=ones[:], rhs=warm_rows[:], start=True, stop=True)
+                nc.tensor.matmul(out=warm_bank[:], lhsT=ones[:, :P], rhs=ones[:], start=True, stop=True)
 
         x_view = x.rearrange("n (p j) h w -> p n (j h w)", j=GROUPS)
         x_raw = keep.tile([P, SAMPLES * GROUPS * PIXELS], BF16)
@@ -142,7 +140,7 @@ def tile_similargcn_pa_kernel(tc, x, weight, W1, b1, out):
 
         def spread_bias():
             bias_bank = psum.tile([P, BANK], F32, tag="bank")
-            nc.tensor.matmul(out=bias_bank[:], lhsT=ones[:], rhs=bias_rows[:], start=True, stop=True)
+            nc.tensor.matmul(out=bias_bank[:], lhsT=ones[:, :P], rhs=bias_rows[:], start=True, stop=True)
             vector_copy(out=bias[:], in_=bias_bank[:])
 
         sorteds, w_tiles, agg_tiles, out_banks, biaseds = {}, {}, {}, {}, {}
@@ -243,17 +241,6 @@ def tile_similargcn_pa_kernel(tc, x, weight, W1, b1, out):
             )
             nc.sync.dma_start(out=out_rounds[i][:, cols], in_=result[:])
 
-        def leaky_store_aside(i, r):
-            cols = slice(r * HIDDEN, (r + 1) * HIDDEN)
-            biased = biaseds[i][:, cols]
-            lift = ends.tile([P, HIDDEN], F32)
-            nc.scalar.activation(
-                out=lift[:], in_=biased, func=mybir.ActivationFunctionType.Relu, scale=SLOPE - 1.0
-            )
-            result = results.tile([P, HIDDEN], F32)
-            nc.gpsimd.tensor_tensor(out=result[:], in0=biased, in1=lift[:], op=ALU.add)
-            nc.sync.dma_start(out=out_rounds[i][:, cols], in_=result[:])
-
         last = ROUNDS
 
         def sort_round(i):
@@ -265,20 +252,23 @@ def tile_similargcn_pa_kernel(tc, x, weight, W1, b1, out):
             turn_weight(i, 0, (scalar_copy, scalar_copy))
             turn_weight(i, 1, (scalar_copy, scalar_copy))
 
-        keep_warm(6)
+        keep_warm(4)
         sort_nodes(0)
+        spread_bias()
         sort_nodes(1)
-        for g in range(PASSES - 1):
-            turn_nodes(g, (scalar_copy, scalar_copy))
-            if g == 0:
-                spread_bias()
-            else:
-                keep_warm(1)
-            if g + 2 < PASSES:
-                sort_nodes(g + 2)
-            quantise_nodes(g)
-        turn_nodes(PASSES - 1, (scalar_copy, vector_copy))
-        quantise_nodes(PASSES - 1)
+        turn_nodes(0, (scalar_copy, scalar_copy))
+        keep_warm(1)
+        sort_nodes(2)
+        turn_nodes(1, (scalar_copy, scalar_copy))
+        keep_warm(1)
+        sort_nodes(3)
+        quantise_nodes(0)
+        quantise_nodes(1)
+        turn_nodes(2, (scalar_copy, scalar_copy))
+        keep_warm(1)
+        quantise_nodes(2)
+        turn_nodes(3, (scalar_copy, vector_copy))
+        quantise_nodes(3)
         turn_weight(0, 0, (scalar_copy, scalar_copy))
         keep_warm(1)
         turn_weight(0, 1, (scalar_copy, scalar_copy))

@@ -232,6 +232,19 @@ def tile_similargcn_pa_kernel(tc, x, weight, W1, b1, out):
                 out=biaseds[i][:, r * HIDDEN : (r + 1) * HIDDEN], in0=out_banks[i, r][:], in1=bias[:], op=ALU.add
             )
 
+        def finish_last(i, r):
+            biased = biaseds[i][:, r * HIDDEN : (r + 1) * HIDDEN]
+            result = results.tile([P, HIDDEN], F32)
+            halves = [slice(h * HIDDEN // 2, (h + 1) * HIDDEN // 2) for h in range(2)]
+            for cols in halves:
+                nc.vector.tensor_tensor(out=biased[:, cols], in0=out_banks[i, r][:, cols], in1=bias[:, cols], op=ALU.add)
+            for h, cols in enumerate(halves):
+                nc.vector.scalar_tensor_tensor(
+                    out=result[:, cols], in0=biased[:, cols], scalar=SLOPE, in1=biased[:, cols], op0=ALU.mult, op1=ALU.max
+                )
+                start = r * HIDDEN + h * HIDDEN // 2
+                nc.sync.dma_start(out=out_rounds[i][:, start : start + HIDDEN // 2], in_=result[:, cols])
+
         def leaky_store(i, r):
             cols = slice(r * HIDDEN, (r + 1) * HIDDEN)
             biased = biaseds[i][:, cols]
@@ -330,5 +343,4 @@ def tile_similargcn_pa_kernel(tc, x, weight, W1, b1, out):
         project(last - 1, 1)
         leaky_store(last - 2, 1)
         leaky_store(last - 1, 0)
-        add_bias(last - 1, 1)
-        leaky_store(last - 1, 1)
+        finish_last(last - 1, 1)

from contextlib import ExitStack

import concourse.mybir as mybir
from concourse.masks import make_identity

F32 = mybir.dt.float32
BF16 = mybir.dt.bfloat16
U32 = mybir.dt.uint32
U8 = mybir.dt.uint8
FP8X4 = mybir.dt.float8_e4m3fn_x4
ALU = mybir.AluOpType

P = 128
PACK = 4
K_PASS = P * PACK
BANK = 512
BANKS = 8

SAMPLES, CHANNELS, PIXELS = 8, 512, 256
NODES = SAMPLES * PIXELS
HIDDEN = 512
FIRST_STEP = 3
SPLIT_ROUNDS = 2
SLOPE = 0.01

PASSES = NODES // K_PASS
GROUPS = CHANNELS // P
TILES = 2
ROUNDS = NODES // (TILES * P)
TILE_CODES = PASSES * P

FLOPS = 2 * NODES * NODES * CHANNELS + 2 * NODES * CHANNELS * HIDDEN


def tile_similargcn_pa_kernel(tc, x, weight, W1, b1, out):
    nc = tc.nc
    with ExitStack() as ctx:
        keep = ctx.enter_context(tc.tile_pool(name="keep", bufs=1))
        raw = ctx.enter_context(tc.tile_pool(name="raw", bufs=ROUNDS))
        work = ctx.enter_context(tc.tile_pool(name="work", bufs=3))
        ends = ctx.enter_context(tc.tile_pool(name="ends", bufs=3))
        results = ctx.enter_context(tc.tile_pool(name="results", bufs=6))
        psum = ctx.enter_context(tc.psum_pool(name="psum", bufs=BANKS))
        ctx.enter_context(tc.manual_schedule())

        ones = keep.tile([P, BANK], BF16)
        nc.gpsimd.memset(ones[:], 1.0)
        ident = keep.tile([P, P], F32)
        make_identity(nc, ident[:])
        bias_rows = keep.tile([P, HIDDEN], BF16)
        nc.vector.memset(bias_rows[:], 0.0)

        def keep_warm(count):
            warm_bank = psum.tile([P, BANK], F32, tag="bank")
            for n in range(count):
                nc.tensor.matmul(out=warm_bank[:], lhsT=ones[:, :P], rhs=ones[:], start=True, stop=True)

        x_view = x.rearrange("n (p j) h w -> p n (j h w)", j=GROUPS)
        x_raw = keep.tile([P, SAMPLES * GROUPS * PIXELS], BF16)
        x_raw_by_sample = x_raw[:].rearrange("p (n f) -> p n f", n=SAMPLES)
        for g in range(PASSES):
            nc.sync.dma_start(out=x_raw_by_sample[:, 2 * g : 2 * g + 2, :], in_=x_view[:, 2 * g : 2 * g + 2, :])
            if g == 0:
                nc.sync.dma_start(out=bias_rows[0:1, :], in_=b1.rearrange("(o h) -> o h", o=1))
        weight_rounds = weight.rearrange("(i p r) k -> i p (r k)", p=P, r=TILES)
        out_rounds = out.rearrange("(i p r) h -> i p (r h)", p=P, r=TILES)
        w1_raw = keep.tile([P, GROUPS * CHANNELS], BF16)
        w_raws = []
        for i in range(ROUNDS):
            w_raw = raw.tile([P, TILES * NODES], BF16)
            if i < SPLIT_ROUNDS:
                for r in range(TILES):
                    cols = slice(r * NODES, (r + 1) * NODES)
                    nc.sync.dma_start(out=w_raw[:, cols], in_=weight_rounds[i][:, cols])
            else:
                nc.sync.dma_start(out=w_raw[:], in_=weight_rounds[i])
            w_raws.append(w_raw)
            if i == 0:
                nc.sync.dma_start(
                    out=w1_raw[:].rearrange("p (a c) -> p a c", a=GROUPS),
                    in_=W1.rearrange("(a p) c -> p a c", p=P),
                )

        def transpose_words(words, first, step):
            bank = psum.tile([P, BANK], F32, tag="bank")
            for q in range(4):
                nc.tensor.transpose(
                    out=bank[:, q * P : (q + 1) * P],
                    in_=words[:, first(q) : first(q) + step * (P - 1) + 1 : step],
                    identity=ident[:],
                )
            return bank

        def pair_up(copy, bank, grouped):
            copy(
                out=grouped.bitcast(F32).rearrange("p (a c u) -> p a c u", a=2, u=2),
                in_=bank[:].rearrange("p (a u c) -> p a c u", a=2, u=2),
            )

        scalar_copy, vector_copy = nc.scalar.copy, nc.vector.tensor_copy

        x_codes = keep.tile([P, PASSES * CHANNELS], U32, align_bytes=64)
        x_scales = keep.tile([P, PASSES * CHANNELS], U8, align_bytes=64)
        x_sorted = [keep.tile([P, 2 * GROUPS * P], F32, name="x_sorted_%d" % g) for g in range(PASSES)]
        x_groupeds = {}

        def sort_nodes(g):
            words = x_raw[:, g * 2 * GROUPS * PIXELS : (g + 1) * 2 * GROUPS * PIXELS].bitcast(F32)
            vector_copy(
                out=x_sorted[g][:].rearrange("p (u j n q) -> p n u j q", u=2, j=GROUPS, n=2),
                in_=words.rearrange("p (n j q u) -> p n u j q", n=2, j=GROUPS, u=2),
            )

        def turn_nodes(g, copies):
            x_grouped = work.tile([P, CHANNELS * PACK], BF16, align_bytes=64)
            for half, copy in enumerate(copies):
                bank = transpose_words(x_sorted[g][:], lambda q: ((q % 2) * GROUPS + 2 * half + q // 2) * P, 1)
                pair_up(copy, bank, x_grouped[:, half * 2 * BANK : (half + 1) * 2 * BANK])
            x_groupeds[g] = x_grouped

        def quantise_nodes(g):
            cols = slice(g * CHANNELS, (g + 1) * CHANNELS)
            nc.vector.quantize_mx(
                out=x_codes[:, cols].bitcast(FP8X4), scales=x_scales[:, cols], in_=x_groupeds[g][:]
            )

        w1_grouped = keep.tile([P, HIDDEN * PACK], BF16, align_bytes=64)
        w1_codes = keep.tile([P, HIDDEN], U32, align_bytes=64)
        w1_scales = keep.tile([P, HIDDEN], U8, align_bytes=64)
        bias = keep.tile([P, HIDDEN], F32)

        def turn_w1(copies):
            w1_words = w1_raw[:].bitcast(F32)
            for half, copy in enumerate(copies):
                bank = transpose_words(w1_words, lambda q: (2 * half + q // 2) * (CHANNELS // 2) + q % 2, 2)
                pair_up(copy, bank, w1_grouped[:, half * 2 * BANK : (half + 1) * 2 * BANK])

        def quantise_w1():
            nc.vector.quantize_mx(out=w1_codes[:].bitcast(FP8X4), scales=w1_scales[:], in_=w1_grouped[:])

        def spread_bias():
            bias_bank = psum.tile([P, BANK], F32, tag="bank")
            nc.tensor.matmul(out=bias_bank[:], lhsT=ones[:, :P], rhs=bias_rows[:], start=True, stop=True)
            vector_copy(out=bias[:], in_=bias_bank[:])

        sorteds, w_tiles, agg_tiles, out_banks, biaseds = {}, {}, {}, {}, {}

        def sort_weight(copy, i, r, halves=(0, 1)):
            if (i, r) not in sorteds:
                sorteds[i, r] = work.tile([P, NODES // 2], F32, name="w_sorted_%d" % r)
            first, last = halves[0], halves[-1] + 1
            words = w_raws[i][:, r * NODES : (r + 1) * NODES].bitcast(F32)
            copy(
                out=sorteds[i, r][:].rearrange("p (u q) -> p u q", u=2)[:, :, first * 2 * P : last * 2 * P],
                in_=words[:, first * BANK : last * BANK].rearrange("p (q u) -> p u q", u=2),
            )

        def turn_weight(i, r, copies):
            w_grouped = work.tile([P, NODES], BF16, align_bytes=64, name="w_grouped_%d" % r)
            w_codes = work.tile([P, TILE_CODES], U32, align_bytes=64, name="w_codes_%d" % r)
            w_scales = work.tile([P, TILE_CODES], U8, align_bytes=64, name="w_scales_%d" % r)
            for half, copy in enumerate(copies):
                if (i, r) in sorteds:
                    bank = transpose_words(
                        sorteds[i, r][:], lambda q: ((q % 2) * PASSES + 2 * half + q // 2) * P, 1
                    )
                else:
                    words = w_raws[i][:, r * NODES : (r + 1) * NODES].bitcast(F32)
                    bank = transpose_words(words, lambda q: (2 * half + q // 2) * 2 * P + q % 2, 2)
                pair_up(copy, bank, w_grouped[:, half * 2 * BANK : (half + 1) * 2 * BANK])
            w_tiles[i, r] = (w_grouped, w_codes, w_scales)

        def quantise_weight(i, r):
            w_grouped, w_codes, w_scales = w_tiles[i, r]
            nc.vector.quantize_mx(out=w_codes[:].bitcast(FP8X4), scales=w_scales[:], in_=w_grouped[:])

        def aggregate(i, r):
            w_grouped, w_codes, w_scales = w_tiles[i, r]
            if i not in agg_tiles:
                agg_grouped = work.tile([P, TILES * P * PACK], BF16, align_bytes=64)
                agg_codes = work.tile([P, TILES * P], U32, align_bytes=64)
                agg_scales = work.tile([P, TILES * P], U8, align_bytes=64)
                agg_tiles[i] = (agg_grouped, agg_codes, agg_scales)
            agg_grouped, agg_codes, agg_scales = agg_tiles[i]
            agg_bank = psum.tile([P, BANK], F32, tag="bank")
            for j in range(GROUPS):
                for g in range(PASSES):
                    x_cols = slice(g * CHANNELS + j * P, g * CHANNELS + (j + 1) * P)
                    w_cols = slice(g * P, (g + 1) * P)
                    nc.tensor.matmul_mx(
                        out=agg_bank[:, j * P : (j + 1) * P],
                        lhsT=x_codes[:, x_cols].bitcast(FP8X4),
                        lhsT_scale=x_scales[:, x_cols],
                        rhs=w_codes[:, w_cols].bitcast(FP8X4),
                        rhs_scale=w_scales[:, w_cols],
                        start=(g == 0),
                        stop=(g == PASSES - 1),
                    )
            scalar_copy(
                out=agg_grouped[:, r * BANK : (r + 1) * BANK].rearrange("p (m j) -> p m j", j=GROUPS),
                in_=agg_bank[:].rearrange("p (j m) -> p m j", j=GROUPS),
            )

        def quantise_agg(i, first=0, count=TILES):
            agg_grouped, agg_codes, agg_scales = agg_tiles[i]
            cols = slice(first * P, (first + count) * P)
            nc.vector.quantize_mx(
                out=agg_codes[:, cols].bitcast(FP8X4),
                scales=agg_scales[:, cols],
                in_=agg_grouped[:, first * BANK : (first + count) * BANK],
            )

        def project(i, r):
            agg_grouped, agg_codes, agg_scales = agg_tiles[i]
            cols = slice(r * P, (r + 1) * P)
            out_bank = psum.tile([P, BANK], F32, tag="bank")
            nc.tensor.matmul_mx(
                out=out_bank[:],
                lhsT=agg_codes[:, cols].bitcast(FP8X4),
                lhsT_scale=agg_scales[:, cols],
                rhs=w1_codes[:].bitcast(FP8X4),
                rhs_scale=w1_scales[:],
                start=True,
                stop=True,
            )
            out_banks[i, r] = out_bank

        def add_bias(i, r):
            if i not in biaseds:
                biaseds[i] = ends.tile([P, TILES * HIDDEN], F32, name="biased")
            nc.vector.tensor_tensor(
                out=biaseds[i][:, r * HIDDEN : (r + 1) * HIDDEN], in0=out_banks[i, r][:], in1=bias[:], op=ALU.add
            )

        def finish_last(i, r):
            biased = biaseds[i][:, r * HIDDEN : (r + 1) * HIDDEN]
            result = results.tile([P, HIDDEN], F32)
            halves = [slice(h * HIDDEN // 2, (h + 1) * HIDDEN // 2) for h in range(2)]
            for cols in halves:
                nc.vector.tensor_tensor(out=biased[:, cols], in0=out_banks[i, r][:, cols], in1=bias[:, cols], op=ALU.add)
            for h, cols in enumerate(halves):
                nc.vector.scalar_tensor_tensor(
                    out=result[:, cols], in0=biased[:, cols], scalar=SLOPE, in1=biased[:, cols], op0=ALU.mult, op1=ALU.max
                )
                start = r * HIDDEN + h * HIDDEN // 2
                nc.sync.dma_start(out=out_rounds[i][:, start : start + HIDDEN // 2], in_=result[:, cols])

        def leaky_store(i, r):
            cols = slice(r * HIDDEN, (r + 1) * HIDDEN)
            biased = biaseds[i][:, cols]
            result = results.tile([P, HIDDEN], F32)
            nc.vector.scalar_tensor_tensor(
                out=result[:], in0=biased, scalar=SLOPE, in1=biased, op0=ALU.mult, op1=ALU.max
            )
            nc.sync.dma_start(out=out_rounds[i][:, cols], in_=result[:])

        last = ROUNDS

        def sort_round(i):
            if i < last:
                sort_weight(vector_copy, i, 0)
                sort_weight(vector_copy if i < FIRST_STEP + 1 else scalar_copy, i, 1)

        def turn_round(i):
            turn_weight(i, 0, (scalar_copy, scalar_copy))
            turn_weight(i, 1, (scalar_copy, scalar_copy))

        keep_warm(4)
        sort_nodes(0)
        spread_bias()
        sort_nodes(1)
        turn_nodes(0, (scalar_copy, scalar_copy))
        keep_warm(1)
        sort_nodes(2)
        turn_nodes(1, (scalar_copy, scalar_copy))
        keep_warm(1)
        sort_nodes(3)
        quantise_nodes(0)
        quantise_nodes(1)
        turn_nodes(2, (scalar_copy, scalar_copy))
        keep_warm(1)
        quantise_nodes(2)
        turn_nodes(3, (scalar_copy, vector_copy))
        quantise_nodes(3)
        turn_weight(0, 0, (scalar_copy, scalar_copy))
        keep_warm(1)
        turn_weight(0, 1, (scalar_copy, scalar_copy))
        quantise_weight(0, 0)
        turn_w1((scalar_copy, scalar_copy))
        sort_weight(vector_copy, 1, 0)
        quantise_weight(0, 1)
        sort_weight(vector_copy, 1, 1)
        aggregate(0, 0)
        quantise_w1()
        aggregate(0, 1)
        turn_round(1)
        sort_weight(vector_copy, 2, 0)
        quantise_agg(0)
        sort_weight(vector_copy, 2, 1)
        quantise_weight(1, 0)
        quantise_weight(1, 1)
        turn_round(2)
        project(0, 0)
        project(0, 1)
        add_bias(0, 0)
        add_bias(0, 1)
        aggregate(1, 0)
        sort_round(3)
        aggregate(1, 1)
        quantise_weight(2, 0)
        sort_round(4)
        quantise_weight(2, 1)

        for i in range(FIRST_STEP, last):
            turn_round(i)
            leaky_store(i - 3, 0)
            quantise_agg(i - 2)
            leaky_store(i - 3, 1)
            sort_round(i + 2)
            quantise_weight(i, 0)
            quantise_weight(i, 1)
            aggregate(i - 1, 0)
            project(i - 2, 0)
            project(i - 2, 1)
            aggregate(i - 1, 1)
            add_bias(i - 2, 0)
            add_bias(i - 2, 1)

        leaky_store(last - 3, 0)
        quantise_agg(last - 2)
        leaky_store(last - 3, 1)
        aggregate(last - 1, 0)
        project(last - 2, 0)
        project(last - 2, 1)
        add_bias(last - 2, 0)
        quantise_agg(last - 1, 0, 1)
        add_bias(last - 2, 1)
        leaky_store(last - 2, 0)
        aggregate(last - 1, 1)
        project(last - 1, 0)
        quantise_agg(last - 1, 1, 1)
        add_bias(last - 1, 0)
        project(last - 1, 1)
        leaky_store(last - 2, 1)
        leaky_store(last - 1, 0)
        finish_last(last - 1, 1)
